import numpy as np
import ml_dtypes


def mxq(x, axis, fmt="e4m3"):
    dtype, down = {"e4m3": (ml_dtypes.float8_e4m3fn, 7), "e5m2": (ml_dtypes.float8_e5m2, 14)}[fmt]
    v = np.moveaxis(np.asarray(x, np.float32).astype(ml_dtypes.bfloat16).astype(np.float64), axis, -1)
    blocks = v.reshape(v.shape[:-1] + (-1, 32))
    amax = np.abs(blocks).max(-1, keepdims=True)
    byte = np.maximum(np.where(amax > 0, np.frexp(amax)[1] - 1 + 127, 0) - down, 1)
    scale = np.exp2(byte - 127.0)
    codes = (blocks / scale).astype(np.float32).astype(dtype).astype(np.float64)
    return np.moveaxis((codes * scale).reshape(v.shape), -1, axis)


WIDE = False


def mx_kscale(k):
    if not WIDE:
        return np.ones(k)
    levels = np.array([10, -10, 5, -5, 0])
    a = np.random.permutation(np.resize(levels, k // 512 * 4)).reshape(k // 512, 4)
    idx = np.arange(k)
    return np.exp2(a[idx // 512, idx % 128 // 32])


BF16 = ml_dtypes.bfloat16


def bf(x):
    return np.asarray(x, np.float32).astype(BF16)


def f64(x):
    return np.asarray(x).astype(np.float64)


E2M1 = np.array([0.0, 0.5, 1.0, 1.5, 2.0, 3.0, 4.0, 6.0, -0.0, -0.5, -1.0, -1.5, -2.0, -3.0, -4.0, -6.0])


def pack_weight(w, fmt):
    k, n = w.shape
    w = f64(bf(w)).reshape(k // 32, 32, n)
    amax = np.abs(w).max(1)
    if fmt == "e4m3":
        byte = np.frexp(amax)[1] - 1 + 127 - 7
    else:
        mant, ex = np.frexp(amax / 6.0)
        byte = np.where(mant > 0.5, ex, ex - 1) + 127
    byte = np.clip(np.where(amax > 0, byte, 1), 1, 254)
    scaled = (w * np.exp2(127.0 - byte)[:, None, :]).reshape(k, n).astype(np.float32)
    by_word = np.ascontiguousarray(scaled.reshape(k // 512, 128, 4, n).transpose(0, 1, 3, 2))
    if fmt == "e4m3":
        words = by_word.astype(ml_dtypes.float8_e4m3fn).view(np.uint8)
    else:
        c = by_word.astype(ml_dtypes.float4_e2m1fn).view(np.uint8) & 0xF
        words = c[..., 0::2] | (c[..., 1::2] << 4)
    return np.ascontiguousarray(words), np.ascontiguousarray(byte.astype(np.uint8).reshape(k // 512, 16, n))


def unpack_weight(words, scales, fmt):
    g, p, n, _ = words.shape
    if fmt == "e4m3":
        vals = np.ascontiguousarray(words).view(ml_dtypes.float8_e4m3fn).astype(np.float64)
    else:
        nib = np.empty((g, p, n, 4), np.uint8)
        nib[..., 0::2] = words & 0xF
        nib[..., 1::2] = words >> 4
        vals = E2M1[nib]
    vals = vals * np.repeat(np.exp2(scales.astype(np.float64) - 127.0), 8, axis=1)[..., None]
    return vals.transpose(0, 1, 3, 2).reshape(g * 512, n)


B, K, N = 1024, 1024, 1024


def setup_inputs():
    s = mx_kscale(K)
    s = s / s.max()
    x = bf(np.random.standard_normal((B, K)) * s)
    W_words, W_scales = pack_weight(np.random.standard_normal((K, N)) * 0.4 / np.sqrt(K) / s[:, None], "e4m3")
    return {"x": x,
            "W_words": W_words,
            "W_scales": W_scales,
            "P": bf(np.random.standard_normal(N) * 0.3),
            "w": bf(0.8 + 0.1 * np.random.standard_normal(1)),
            "p": bf(0.5 + 0.1 * np.random.standard_normal(1)),
            "sine_w": bf(1.2 + 0.1 * np.random.standard_normal(1)),
            "cosine_w": bf(-0.7 + 0.1 * np.random.standard_normal(1))}


def reference(x, W_words, W_scales, P, w, p, sine_w, cosine_w):
    x = f64(x)
    original = f64(w) * x + f64(p)
    z = (mxq(x, 1, "e4m3") @ unpack_weight(W_words, W_scales, "e4m3")) + f64(P)
    periodic = f64(sine_w) * np.sin(z) + f64(cosine_w) * np.cos(z)
    return np.concatenate((original, periodic), axis=-1)

@@ -1,0 +1,316 @@
+import math
+from contextlib import ExitStack
+
+import concourse.mybir as mybir
+from concourse.masks import make_identity
+
+F32 = mybir.dt.float32
+BF16 = mybir.dt.bfloat16
+I32 = mybir.dt.int32
+U32 = mybir.dt.uint32
+U8 = mybir.dt.uint8
+FP8X4 = mybir.dt.float8_e4m3fn_x4
+ALU = mybir.AluOpType
+ACT = mybir.ActivationFunctionType
+
+P128 = 128
+ROWS = 1024
+K = 1024
+COLS = 1024
+PACK = 4
+K_PASS = P128 * PACK
+PASSES = K // K_PASS
+ROW_TILES = ROWS // P128
+CHUNK_TILES = 4
+CHUNK = CHUNK_TILES * P128
+CHUNKS = ROW_TILES // CHUNK_TILES
+COL_TILES = COLS // P128
+STORE_TILES = 2
+LOAD_TILES = 2
+W_LOADS = 2
+W_LOAD_COLS = COLS // W_LOADS
+W_LOAD_TILES = COL_TILES // W_LOADS
+
+HALF_PI = math.pi / 2.0
+TWO_PI = 2.0 * math.pi
+TINY = 1.2e-38
+
+FLOPS = 2 * ROWS * K * COLS
+
+
+def turn_back(nc, column, vector, angle, complement, tag):
+    sin_a = column("sin_" + tag)
+    cos_a = column("cos_" + tag)
+    nc.scalar.activation(out=sin_a[:], in_=angle[:], func=ACT.Sin)
+    nc.scalar.activation(out=cos_a[:], in_=complement[:], func=ACT.Sin)
+    across = column("across_" + tag)
+    along = column("along_" + tag)
+    nc.vector.tensor_mul(out=across[:], in0=vector["abs_cosine"][:], in1=cos_a[:])
+    nc.vector.scalar_tensor_tensor(
+        out=across[:], in0=sin_a[:], scalar=vector["neg_sine"][:, 0:1], in1=across[:], op0=ALU.mult, op1=ALU.add
+    )
+    nc.vector.tensor_mul(out=along[:], in0=vector["sine"][:], in1=cos_a[:])
+    nc.vector.scalar_tensor_tensor(
+        out=along[:], in0=sin_a[:], scalar=vector["abs_cosine"][:, 0:1], in1=along[:], op0=ALU.mult, op1=ALU.add
+    )
+    return across, along
+
+
+def angle_of(nc, column, vector):
+    norm1 = column("norm1")
+    ratio = column("ratio")
+    guess = column("guess")
+    guess_complement = column("guess_complement")
+    nc.vector.tensor_scalar(
+        out=norm1[:], in0=vector["abs_sine"][:], scalar1=vector["abs_cosine"][:, 0:1], scalar2=TINY,
+        op0=ALU.add, op1=ALU.max,
+    )
+    nc.vector.reciprocal(out=norm1[:], in_=norm1[:])
+    nc.vector.tensor_mul(out=ratio[:], in0=vector["sine"][:], in1=norm1[:])
+    nc.vector.tensor_scalar(
+        out=guess[:], in0=ratio[:], scalar1=-HALF_PI, scalar2=HALF_PI, op0=ALU.mult, op1=ALU.add
+    )
+    nc.vector.tensor_scalar_mul(out=guess_complement[:], in0=ratio[:], scalar1=HALF_PI)
+
+    across, along = turn_back(nc, column, vector, guess, guess_complement, "guess")
+    tangent = column("tangent")
+    square = column("square")
+    series = column("series")
+    nc.vector.tensor_scalar_max(out=along[:], in0=along[:], scalar1=TINY)
+    nc.vector.reciprocal(out=along[:], in_=along[:])
+    nc.vector.tensor_mul(out=tangent[:], in0=across[:], in1=along[:])
+    nc.vector.tensor_mul(out=square[:], in0=tangent[:], in1=tangent[:])
+    nc.vector.tensor_scalar(
+        out=series[:], in0=square[:], scalar1=-1.0 / 7.0, scalar2=1.0 / 5.0, op0=ALU.mult, op1=ALU.add
+    )
+    for coefficient in (-1.0 / 3.0, 1.0):
+        nc.vector.tensor_scalar(
+            out=series[:], in0=series[:], scalar1=square[:, 0:1], scalar2=coefficient, op0=ALU.mult, op1=ALU.add
+        )
+    angle = column("angle")
+    complement = column("complement")
+    nc.vector.scalar_tensor_tensor(
+        out=angle[:], in0=series[:], scalar=tangent[:, 0:1], in1=guess[:], op0=ALU.mult, op1=ALU.add
+    )
+    nc.vector.tensor_scalar(
+        out=complement[:], in0=angle[:], scalar1=-1.0, scalar2=HALF_PI, op0=ALU.mult, op1=ALU.add
+    )
+    return angle, complement
+
+
+def tile_time2vec_kernel(tc, x, W_words, W_scales, P, w, p, sine_w, cosine_w, out):
+    nc = tc.nc
+    with ExitStack() as ctx:
+        consts = ctx.enter_context(tc.tile_pool(name="consts", bufs=1))
+        keep = ctx.enter_context(tc.tile_pool(name="keep", bufs=1))
+        work = ctx.enter_context(tc.tile_pool(name="work", bufs=3))
+        outgoing = ctx.enter_context(tc.tile_pool(name="outgoing", bufs=4))
+        psum = ctx.enter_context(tc.psum_pool(name="psum", bufs=1))
+        ctx.enter_context(tc.manual_schedule())
+
+        def column(name):
+            return consts.tile([P128, 1], F32, name=name)
+
+        x_rows = x.rearrange("(p i) k -> p i k", i=ROW_TILES)
+        out_rows = out.rearrange("(p i) c -> p i c", i=ROW_TILES)
+
+        x_sb = keep.tile([P128, ROW_TILES, K], BF16)
+        x_pairs = x_sb[:].bitcast(F32)
+        w_codes = keep.tile([P128, W_LOADS, PASSES, W_LOAD_COLS], U32, align_bytes=64)
+        w_planes = keep.tile([P128, PASSES, COLS], U8, align_bytes=64)
+        x_codes = keep.tile([P128, CHUNKS, PASSES, CHUNK], U32, align_bytes=64)
+        x_planes = keep.tile([P128, CHUNKS, PASSES, CHUNK], U8, align_bytes=64)
+
+        nc.vector.memset(w_planes[:].bitcast(I32), 0)
+        p_rows_bf = consts.tile([P128, P128], BF16)
+        nc.vector.memset(p_rows_bf[:], 0.0)
+        zero = column("zero")
+        nc.vector.memset(zero[:], 0.0)
+
+        nc.scalar.dma_start(out=p_rows_bf[0:COL_TILES, :], in_=P.rearrange("(j n) -> j n", n=P128))
+        raw = {}
+        for name, source, queue in (
+            ("sine", sine_w, nc.sync), ("cosine", cosine_w, nc.sync), ("w", w, nc.scalar), ("p", p, nc.scalar)
+        ):
+            raw[name] = consts.tile([P128, 1], BF16, name=name + "_bf")
+            queue.dma_start(out=raw[name][:], in_=source.partition_broadcast(P128))
+
+        def load_x(first_tile):
+            tiles = slice(first_tile, first_tile + LOAD_TILES)
+            nc.sync.dma_start(out=x_sb[:, tiles, :], in_=x_rows[:, tiles, :])
+
+        load_x(0)
+        load_x(2)
+        for quadrant in range(4):
+            nc.sync.dma_start(
+                out=w_planes[32 * quadrant : 32 * quadrant + 4].bitcast(I32),
+                in_=W_scales[:, 4 * quadrant : 4 * quadrant + 4, :].rearrange("g r n -> r g n").bitcast(I32),
+            )
+        w_words = W_words.rearrange("g q n t -> q g (n t)").bitcast(I32)
+        for part in range(W_LOADS):
+            cols = slice(part * W_LOAD_COLS, (part + 1) * W_LOAD_COLS)
+            nc.sync.dma_start(out=w_codes[:, part].bitcast(I32), in_=w_words[:, :, cols])
+        load_x(4)
+        load_x(6)
+
+        table_warm = column("table_warm")
+        nc.scalar.activation(out=table_warm[:], in_=zero[:], func=ACT.Sin)
+
+        identity = consts.tile([P128, P128], F32)
+        make_identity(nc, identity[:])
+
+        small = {}
+        for name in ("sine", "cosine", "w", "p"):
+            small[name] = column(name)
+            nc.vector.tensor_copy(out=small[name][:], in_=raw[name][:])
+
+        p_rows = consts.tile([P128, P128], F32)
+        nc.vector.tensor_copy(out=p_rows[:], in_=p_rows_bf[:])
+        p_cols = psum.tile([P128, CHUNK_TILES, P128], F32, tag="back", bufs=3)
+        nc.tensor.transpose(p_cols[:, 0, :], p_rows[:], identity[:])
+
+        vector = {"sine": small["sine"]}
+        for name, source in (("abs_sine", "sine"), ("abs_cosine", "cosine")):
+            vector[name] = column(name)
+            nc.vector.scalar_tensor_tensor(
+                out=vector[name][:], in0=small[source][:], scalar=-1.0, in1=small[source][:],
+                op0=ALU.mult, op1=ALU.max,
+            )
+        vector["neg_sine"] = column("neg_sine")
+        nc.vector.tensor_scalar_mul(out=vector["neg_sine"][:], in0=small["sine"][:], scalar1=-1.0)
+        angle, complement = angle_of(nc, column, vector)
+        half_sign = column("half_sign")
+        phase = column("phase")
+        nc.vector.tensor_scalar(
+            out=half_sign[:], in0=small["cosine"][:], scalar1=0.0, scalar2=0.5, op0=ALU.is_ge, op1=ALU.subtract
+        )
+        nc.vector.tensor_scalar(
+            out=phase[:], in0=angle[:], scalar1=half_sign[:, 0:1], scalar2=2.0, op0=ALU.mult, op1=ALU.mult
+        )
+        bias = consts.tile([P128, COL_TILES], F32)
+        bias_turns = consts.tile([P128, COL_TILES], F32)
+        nc.vector.tensor_scalar_add(out=bias[:], in0=p_cols[:, 0, 0:COL_TILES], scalar1=phase[:, 0:1])
+        nc.vector.tensor_scalar_mul(out=bias_turns[:], in0=bias[:], scalar1=1.0 / TWO_PI)
+
+        def linear_term(first_tile):
+            tiles = slice(first_tile, first_tile + LOAD_TILES)
+            linear = outgoing.tile([P128, LOAD_TILES, K], F32)
+            nc.gpsimd.tensor_scalar(
+                out=linear[:], in0=x_sb[:, tiles, :],
+                scalar1=small["w"][:, 0:1], scalar2=small["p"][:, 0:1], op0=ALU.mult, op1=ALU.add,
+            )
+            nc.sync.dma_start(out=out_rows[:, tiles, 0:K], in_=linear[:])
+
+        def quantise_row_tile(i):
+            c, local = divmod(i, CHUNK_TILES)
+            cols = slice(local * P128, (local + 1) * P128)
+            xt = psum.tile([P128, PACK, P128], F32, tag="xt", bufs=2)
+            for g in range(PASSES):
+                for u in range(2):
+                    nc.tensor.transpose(
+                        xt[:, 2 * g + u, :],
+                        x_pairs[:, i, 256 * g + u : 256 * (g + 1) : 2],
+                        identity[:],
+                    )
+            grouped = work.tile([P128, PASSES, P128, PACK], BF16, align_bytes=64)
+            nc.scalar.copy(out=grouped[:].bitcast(F32), in_=xt[:].rearrange("q (g u) b -> q g b u", u=2))
+            for g in range(PASSES):
+                nc.vector.quantize_mx(
+                    out=x_codes[:, c, g, cols].bitcast(FP8X4),
+                    scales=x_planes[:, c, g, cols],
+                    in_=grouped[:, g].rearrange("q b t -> q (b t)"),
+                )
+
+        steps = CHUNKS * COL_TILES
+        z_of = {}
+        reduced_of = {}
+        wave_of = {}
+        back_of = {}
+        periodic_of = {}
+
+        def multiply(step):
+            c, j = divmod(step, COL_TILES)
+            n_cols = slice(j * P128, (j + 1) * P128)
+            part, part_tile = divmod(j, W_LOAD_TILES)
+            part_cols = slice(part_tile * P128, (part_tile + 1) * P128)
+            z = psum.tile([P128, CHUNK], F32, tag="z", bufs=3)
+            for g in range(PASSES):
+                nc.tensor.matmul_mx(
+                    out=z[:],
+                    lhsT=w_codes[:, part, g, part_cols].bitcast(FP8X4),
+                    lhsT_scale=w_planes[:, g, n_cols],
+                    rhs=x_codes[:, c, g, :].bitcast(FP8X4),
+                    rhs_scale=x_planes[:, c, g, :],
+                    start=(g == 0),
+                    stop=(g == PASSES - 1),
+                )
+            z_of[step] = z
+
+        def reduce_range(step):
+            j = step % COL_TILES
+            z = z_of[step]
+            turns = work.tile([P128, CHUNK], I32)
+            nc.vector.tensor_scalar(
+                out=turns[:], in0=z[:], scalar1=1.0 / TWO_PI, scalar2=bias_turns[:, j : j + 1],
+                op0=ALU.mult, op1=ALU.add,
+            )
+            reduced = work.tile([P128, CHUNK], F32)
+            nc.vector.scalar_tensor_tensor(
+                out=reduced[:], in0=turns[:], scalar=-TWO_PI, in1=z[:], op0=ALU.mult, op1=ALU.add
+            )
+            reduced_of[step] = reduced
+
+        def sine(step):
+            j = step % COL_TILES
+            wave = work.tile([P128, CHUNK], F32)
+            nc.scalar.activation(
+                out=wave[:], in_=reduced_of[step][:], func=ACT.Sin, bias=bias[:, j : j + 1], scale=1.0
+            )
+            wave_of[step] = wave
+
+        def turn_to_rows(step):
+            back = psum.tile([P128, CHUNK_TILES, P128], F32, tag="back", bufs=3)
+            for local in range(CHUNK_TILES):
+                nc.tensor.transpose(
+                    back[:, local, :], wave_of[step][:, local * P128 : (local + 1) * P128], identity[:]
+                )
+            back_of[step] = back
+
+        def scale_and_store(step):
+            c, j = divmod(step, COL_TILES)
+            tiles = slice(c * CHUNK_TILES, (c + 1) * CHUNK_TILES)
+            place = j % STORE_TILES
+            if place == 0:
+                periodic = outgoing.tile([P128, CHUNK_TILES, STORE_TILES * P128], F32)
+                periodic_of[step // STORE_TILES] = periodic
+            periodic = periodic_of[step // STORE_TILES]
+            nc.scalar.activation(
+                out=periodic[:, :, place * P128 : (place + 1) * P128], in_=back_of[step][:],
+                func=ACT.Copy, scale=amplitude[:, 0:1],
+            )
+            if place == STORE_TILES - 1:
+                first = K + (j + 1 - STORE_TILES) * P128
+                nc.sync.dma_start(out=out_rows[:, tiles, first : first + STORE_TILES * P128], in_=periodic[:])
+
+        for i in range(CHUNK_TILES):
+            quantise_row_tile(i)
+        for first_tile in range(0, CHUNK_TILES, LOAD_TILES):
+            linear_term(first_tile)
+        amplitude = turn_back(nc, column, vector, angle, complement, "angle")[1]
+
+        multiply(0)
+        for s in range(steps + 2):
+            if s >= 2:
+                turn_to_rows(s - 2)
+            if s + 1 < steps:
+                multiply(s + 1)
+            if s < steps:
+                reduce_range(s)
+            if 1 <= s <= steps:
+                sine(s - 1)
+            if s >= 2:
+                scale_and_store(s - 2)
+            if 1 <= s <= CHUNK_TILES:
+                quantise_row_tile(CHUNK_TILES + s - 1)
+                if s % LOAD_TILES == 0:
+                    linear_term(CHUNK_TILES + s - LOAD_TILES)

@@ -30,6 +30,10 @@ LOAD_TILES = 2
 W_LOADS = 2
 W_LOAD_COLS = COLS // W_LOADS
 W_LOAD_TILES = COL_TILES // W_LOADS
+SCALARS = ("sine", "cosine", "w", "p")
+SCALAR_STEP = 16
+SPREAD_P = 32
+SPREAD_SCALARS = 64
 
 HALF_PI = math.pi / 2.0
 TWO_PI = 2.0 * math.pi
@@ -122,18 +126,21 @@ def tile_time2vec_kernel(tc, x, W_words, W_scales, P, w, p, sine_w, cosine_w, ou
         x_planes = keep.tile([P128, CHUNKS, PASSES, CHUNK], U8, align_bytes=64)
 
         nc.vector.memset(w_planes[:].bitcast(I32), 0)
-        p_rows_bf = consts.tile([P128, P128], BF16)
-        nc.vector.memset(p_rows_bf[:], 0.0)
         zero = column("zero")
         nc.vector.memset(zero[:], 0.0)
 
-        nc.scalar.dma_start(out=p_rows_bf[0:COL_TILES, :], in_=P.rearrange("(j n) -> j n", n=P128))
-        raw = {}
-        for name, source, queue in (
-            ("sine", sine_w, nc.sync), ("cosine", cosine_w, nc.sync), ("w", w, nc.scalar), ("p", p, nc.scalar)
-        ):
-            raw[name] = consts.tile([P128, 1], BF16, name=name + "_bf")
-            queue.dma_start(out=raw[name][:], in_=source.partition_broadcast(P128))
+        p_rows = consts.tile([P128, P128], BF16)
+        scalar_row = consts.tile([P128, len(SCALARS) * SCALAR_STEP], BF16)
+        ones = consts.tile([P128, P128], BF16)
+        nc.gpsimd.memset(scalar_row[:].bitcast(F32), 0.0)
+        nc.gpsimd.memset(p_rows[:].bitcast(F32), 0.0)
+        nc.gpsimd.memset(ones[:], 1.0)
+        for place, source in enumerate((sine_w, cosine_w, w, p)):
+            nc.scalar.dma_start(
+                out=scalar_row[0:1, place * SCALAR_STEP : place * SCALAR_STEP + 1],
+                in_=source.rearrange("(o n) -> o n", o=1),
+            )
+        nc.scalar.dma_start(out=p_rows[0:COL_TILES, :], in_=P.rearrange("(j n) -> j n", n=P128))
 
         def load_x(first_tile):
             tiles = slice(first_tile, first_tile + LOAD_TILES)
@@ -159,15 +166,21 @@ def tile_time2vec_kernel(tc, x, W_words, W_scales, P, w, p, sine_w, cosine_w, ou
         identity = consts.tile([P128, P128], F32)
         make_identity(nc, identity[:])
 
+        identity_bf = consts.tile([P128, SPREAD_P], BF16)
+        nc.vector.tensor_copy(out=identity_bf[:], in_=identity[:, 0:SPREAD_P])
+        spread = psum.tile([P128, CHUNK], F32, tag="back", bufs=3)
+        nc.tensor.matmul(
+            out=spread[:, SPREAD_SCALARS : SPREAD_SCALARS + len(SCALARS) * SCALAR_STEP],
+            lhsT=ones[:], rhs=scalar_row[:], start=True, stop=True,
+        )
+        nc.tensor.matmul(out=spread[:, 0:SPREAD_P], lhsT=p_rows[:], rhs=identity_bf[:], start=True, stop=True)
+        scalars = consts.tile([P128, len(SCALARS)], F32)
+        nc.vector.tensor_copy(
+            out=scalars[:], in_=spread[:, SPREAD_SCALARS : SPREAD_SCALARS + len(SCALARS) * SCALAR_STEP : SCALAR_STEP]
+        )
         small = {}
-        for name in ("sine", "cosine", "w", "p"):
-            small[name] = column(name)
-            nc.vector.tensor_copy(out=small[name][:], in_=raw[name][:])
-
-        p_rows = consts.tile([P128, P128], F32)
-        nc.vector.tensor_copy(out=p_rows[:], in_=p_rows_bf[:])
-        p_cols = psum.tile([P128, CHUNK_TILES, P128], F32, tag="back", bufs=3)
-        nc.tensor.transpose(p_cols[:, 0, :], p_rows[:], identity[:])
+        for place, name in enumerate(SCALARS):
+            small[name] = scalars[:, place : place + 1]
 
         vector = {"sine": small["sine"]}
         for name, source in (("abs_sine", "sine"), ("abs_cosine", "cosine")):
@@ -189,7 +202,7 @@ def tile_time2vec_kernel(tc, x, W_words, W_scales, P, w, p, sine_w, cosine_w, ou
         )
         bias = consts.tile([P128, COL_TILES], F32)
         bias_turns = consts.tile([P128, COL_TILES], F32)
-        nc.vector.tensor_scalar_add(out=bias[:], in0=p_cols[:, 0, 0:COL_TILES], scalar1=phase[:, 0:1])
+        nc.vector.tensor_scalar_add(out=bias[:], in0=spread[:, 0:COL_TILES], scalar1=phase[:, 0:1])
         nc.vector.tensor_scalar_mul(out=bias_turns[:], in0=bias[:], scalar1=1.0 / TWO_PI)
 
         def linear_term(first_tile):
@@ -197,7 +210,7 @@ def tile_time2vec_kernel(tc, x, W_words, W_scales, P, w, p, sine_w, cosine_w, ou
             linear = outgoing.tile([P128, LOAD_TILES, K], F32)
             nc.gpsimd.tensor_scalar(
                 out=linear[:], in0=x_sb[:, tiles, :],
-                scalar1=small["w"][:, 0:1], scalar2=small["p"][:, 0:1], op0=ALU.mult, op1=ALU.add,
+                scalar1=w_and_p[:, 0:1], scalar2=w_and_p[:, 1:2], op0=ALU.mult, op1=ALU.add,
             )
             nc.sync.dma_start(out=out_rows[:, tiles, 0:K], in_=linear[:])
 
@@ -294,10 +307,9 @@ def tile_time2vec_kernel(tc, x, W_words, W_scales, P, w, p, sine_w, cosine_w, ou
 
         for i in range(CHUNK_TILES):
             quantise_row_tile(i)
-        for first_tile in range(0, CHUNK_TILES, LOAD_TILES):
-            linear_term(first_tile)
         amplitude = turn_back(nc, column, vector, angle, complement, "angle")[1]
 
+        w_and_p = consts.tile([P128, 2], F32)
         multiply(0)
         for s in range(steps + 2):
             if s >= 2:
@@ -312,5 +324,7 @@ def tile_time2vec_kernel(tc, x, W_words, W_scales, P, w, p, sine_w, cosine_w, ou
                 scale_and_store(s - 2)
             if 1 <= s <= CHUNK_TILES:
                 quantise_row_tile(CHUNK_TILES + s - 1)
-                if s % LOAD_TILES == 0:
-                    linear_term(CHUNK_TILES + s - LOAD_TILES)
+            if s == CHUNK_TILES:
+                nc.vector.tensor_copy(out=w_and_p[:], in_=scalars[:, 2:4])
+            if s > CHUNK_TILES and (s - CHUNK_TILES) % 2 == 1 and (s - CHUNK_TILES) // 2 < ROW_TILES // LOAD_TILES:
+                linear_term(LOAD_TILES * ((s - CHUNK_TILES) // 2))

@@ -27,6 +27,8 @@ CHUNKS = ROW_TILES // CHUNK_TILES
 COL_TILES = COLS // P128
 STORE_TILES = 2
 LOAD_TILES = 2
+LOADS = ROW_TILES // LOAD_TILES
+PSUM_BANKS = 8
 W_LOADS = 2
 W_LOAD_COLS = COLS // W_LOADS
 W_LOAD_TILES = COL_TILES // W_LOADS
@@ -49,9 +51,10 @@ def turn_back(nc, column, vector, angle, complement, tag):
     nc.scalar.activation(out=cos_a[:], in_=complement[:], func=ACT.Sin)
     across = column("across_" + tag)
     along = column("along_" + tag)
-    nc.vector.tensor_mul(out=across[:], in0=vector["abs_cosine"][:], in1=cos_a[:])
+    nc.vector.tensor_mul(out=across[:], in0=vector["sine"][:], in1=sin_a[:])
     nc.vector.scalar_tensor_tensor(
-        out=across[:], in0=sin_a[:], scalar=vector["neg_sine"][:, 0:1], in1=across[:], op0=ALU.mult, op1=ALU.add
+        out=across[:], in0=cos_a[:], scalar=vector["abs_cosine"][:, 0:1], in1=across[:],
+        op0=ALU.mult, op1=ALU.subtract,
     )
     nc.vector.tensor_mul(out=along[:], in0=vector["sine"][:], in1=cos_a[:])
     nc.vector.scalar_tensor_tensor(
@@ -107,9 +110,10 @@ def tile_time2vec_kernel(tc, x, W_words, W_scales, P, w, p, sine_w, cosine_w, ou
     with ExitStack() as ctx:
         consts = ctx.enter_context(tc.tile_pool(name="consts", bufs=1))
         keep = ctx.enter_context(tc.tile_pool(name="keep", bufs=1))
-        work = ctx.enter_context(tc.tile_pool(name="work", bufs=3))
+        stage = ctx.enter_context(tc.tile_pool(name="stage", bufs=ROW_TILES))
+        work = ctx.enter_context(tc.tile_pool(name="work", bufs=4))
         outgoing = ctx.enter_context(tc.tile_pool(name="outgoing", bufs=4))
-        psum = ctx.enter_context(tc.psum_pool(name="psum", bufs=1))
+        psum = ctx.enter_context(tc.psum_pool(name="psum", bufs=PSUM_BANKS))
         ctx.enter_context(tc.manual_schedule())
 
         def column(name):
@@ -135,19 +139,18 @@ def tile_time2vec_kernel(tc, x, W_words, W_scales, P, w, p, sine_w, cosine_w, ou
         nc.gpsimd.memset(scalar_row[:].bitcast(F32), 0.0)
         nc.gpsimd.memset(p_rows[:].bitcast(F32), 0.0)
         nc.gpsimd.memset(ones[:], 1.0)
-        for place, source in enumerate((sine_w, cosine_w, w, p)):
-            nc.scalar.dma_start(
+        for place, source, queue in (
+            (0, sine_w, nc.sync), (2, w, nc.scalar), (1, cosine_w, nc.sync), (3, p, nc.scalar)
+        ):
+            queue.dma_start(
                 out=scalar_row[0:1, place * SCALAR_STEP : place * SCALAR_STEP + 1],
                 in_=source.rearrange("(o n) -> o n", o=1),
             )
-        nc.scalar.dma_start(out=p_rows[0:COL_TILES, :], in_=P.rearrange("(j n) -> j n", n=P128))
+        nc.sync.dma_start(out=p_rows[0:COL_TILES, :], in_=P.rearrange("(j n) -> j n", n=P128))
 
-        def load_x(first_tile):
+        for first_tile in range(0, ROW_TILES, LOAD_TILES):
             tiles = slice(first_tile, first_tile + LOAD_TILES)
             nc.sync.dma_start(out=x_sb[:, tiles, :], in_=x_rows[:, tiles, :])
-
-        load_x(0)
-        load_x(2)
         for quadrant in range(4):
             nc.sync.dma_start(
                 out=w_planes[32 * quadrant : 32 * quadrant + 4].bitcast(I32),
@@ -157,8 +160,6 @@ def tile_time2vec_kernel(tc, x, W_words, W_scales, P, w, p, sine_w, cosine_w, ou
         for part in range(W_LOADS):
             cols = slice(part * W_LOAD_COLS, (part + 1) * W_LOAD_COLS)
             nc.sync.dma_start(out=w_codes[:, part].bitcast(I32), in_=w_words[:, :, cols])
-        load_x(4)
-        load_x(6)
 
         table_warm = column("table_warm")
         nc.scalar.activation(out=table_warm[:], in_=zero[:], func=ACT.Sin)
@@ -168,7 +169,7 @@ def tile_time2vec_kernel(tc, x, W_words, W_scales, P, w, p, sine_w, cosine_w, ou
 
         identity_bf = consts.tile([P128, SPREAD_P], BF16)
         nc.vector.tensor_copy(out=identity_bf[:], in_=identity[:, 0:SPREAD_P])
-        spread = psum.tile([P128, CHUNK], F32, tag="back", bufs=3)
+        spread = psum.tile([P128, CHUNK], F32, tag="bank")
         nc.tensor.matmul(
             out=spread[:, SPREAD_SCALARS : SPREAD_SCALARS + len(SCALARS) * SCALAR_STEP],
             lhsT=ones[:], rhs=scalar_row[:], start=True, stop=True,
@@ -189,8 +190,6 @@ def tile_time2vec_kernel(tc, x, W_words, W_scales, P, w, p, sine_w, cosine_w, ou
                 out=vector[name][:], in0=small[source][:], scalar=-1.0, in1=small[source][:],
                 op0=ALU.mult, op1=ALU.max,
             )
-        vector["neg_sine"] = column("neg_sine")
-        nc.vector.tensor_scalar_mul(out=vector["neg_sine"][:], in0=small["sine"][:], scalar1=-1.0)
         angle, complement = angle_of(nc, column, vector)
         half_sign = column("half_sign")
         phase = column("phase")
@@ -205,27 +204,16 @@ def tile_time2vec_kernel(tc, x, W_words, W_scales, P, w, p, sine_w, cosine_w, ou
         nc.vector.tensor_scalar_add(out=bias[:], in0=spread[:, 0:COL_TILES], scalar1=phase[:, 0:1])
         nc.vector.tensor_scalar_mul(out=bias_turns[:], in0=bias[:], scalar1=1.0 / TWO_PI)
 
-        def linear_term(first_tile):
-            tiles = slice(first_tile, first_tile + LOAD_TILES)
-            linear = outgoing.tile([P128, LOAD_TILES, K], F32)
-            nc.gpsimd.tensor_scalar(
-                out=linear[:], in0=x_sb[:, tiles, :],
-                scalar1=w_and_p[:, 0:1], scalar2=w_and_p[:, 1:2], op0=ALU.mult, op1=ALU.add,
-            )
-            nc.sync.dma_start(out=out_rows[:, tiles, 0:K], in_=linear[:])
-
-        def quantise_row_tile(i):
+        for i in range(ROW_TILES):
             c, local = divmod(i, CHUNK_TILES)
             cols = slice(local * P128, (local + 1) * P128)
-            xt = psum.tile([P128, PACK, P128], F32, tag="xt", bufs=2)
+            xt = psum.tile([P128, PACK, P128], F32, tag="bank")
             for g in range(PASSES):
                 for u in range(2):
                     nc.tensor.transpose(
-                        xt[:, 2 * g + u, :],
-                        x_pairs[:, i, 256 * g + u : 256 * (g + 1) : 2],
-                        identity[:],
+                        xt[:, 2 * g + u, :], x_pairs[:, i, 256 * g + u : 256 * (g + 1) : 2], identity[:]
                     )
-            grouped = work.tile([P128, PASSES, P128, PACK], BF16, align_bytes=64)
+            grouped = stage.tile([P128, PASSES, P128, PACK], BF16, align_bytes=64)
             nc.scalar.copy(out=grouped[:].bitcast(F32), in_=xt[:].rearrange("q (g u) b -> q g b u", u=2))
             for g in range(PASSES):
                 nc.vector.quantize_mx(
@@ -233,6 +221,26 @@ def tile_time2vec_kernel(tc, x, W_words, W_scales, P, w, p, sine_w, cosine_w, ou
                     scales=x_planes[:, c, g, cols],
                     in_=grouped[:, g].rearrange("q b t -> q (b t)"),
                 )
+            if i == CHUNK_TILES - 1:
+                amplitude = turn_back(nc, column, vector, angle, complement, "angle")[1]
+
+        w_and_p = consts.tile([P128, 2], F32)
+        nc.vector.tensor_copy(out=w_and_p[:], in_=scalars[:, 2:4])
+
+        linear_of = {}
+
+        def linear_term(load):
+            tiles = slice(load * LOAD_TILES, (load + 1) * LOAD_TILES)
+            linear = outgoing.tile([P128, LOAD_TILES, K], F32)
+            nc.gpsimd.tensor_scalar(
+                out=linear[:], in0=x_sb[:, tiles, :],
+                scalar1=w_and_p[:, 0:1], scalar2=w_and_p[:, 1:2], op0=ALU.mult, op1=ALU.add,
+            )
+            linear_of[load] = linear
+
+        def store_linear(load):
+            tiles = slice(load * LOAD_TILES, (load + 1) * LOAD_TILES)
+            nc.sync.dma_start(out=out_rows[:, tiles, 0:K], in_=linear_of[load][:])
 
         steps = CHUNKS * COL_TILES
         z_of = {}
@@ -246,7 +254,7 @@ def tile_time2vec_kernel(tc, x, W_words, W_scales, P, w, p, sine_w, cosine_w, ou
             n_cols = slice(j * P128, (j + 1) * P128)
             part, part_tile = divmod(j, W_LOAD_TILES)
             part_cols = slice(part_tile * P128, (part_tile + 1) * P128)
-            z = psum.tile([P128, CHUNK], F32, tag="z", bufs=3)
+            z = psum.tile([P128, CHUNK], F32, tag="bank")
             for g in range(PASSES):
                 nc.tensor.matmul_mx(
                     out=z[:],
@@ -282,7 +290,7 @@ def tile_time2vec_kernel(tc, x, W_words, W_scales, P, w, p, sine_w, cosine_w, ou
             wave_of[step] = wave
 
         def turn_to_rows(step):
-            back = psum.tile([P128, CHUNK_TILES, P128], F32, tag="back", bufs=3)
+            back = psum.tile([P128, CHUNK_TILES, P128], F32, tag="bank")
             for local in range(CHUNK_TILES):
                 nc.tensor.transpose(
                     back[:, local, :], wave_of[step][:, local * P128 : (local + 1) * P128], identity[:]
@@ -305,26 +313,20 @@ def tile_time2vec_kernel(tc, x, W_words, W_scales, P, w, p, sine_w, cosine_w, ou
                 first = K + (j + 1 - STORE_TILES) * P128
                 nc.sync.dma_start(out=out_rows[:, tiles, first : first + STORE_TILES * P128], in_=periodic[:])
 
-        for i in range(CHUNK_TILES):
-            quantise_row_tile(i)
-        amplitude = turn_back(nc, column, vector, angle, complement, "angle")[1]
-
-        w_and_p = consts.tile([P128, 2], F32)
         multiply(0)
+        multiply(1)
         for s in range(steps + 2):
             if s >= 2:
                 turn_to_rows(s - 2)
-            if s + 1 < steps:
-                multiply(s + 1)
+            if s + 2 < steps:
+                multiply(s + 2)
             if s < steps:
                 reduce_range(s)
             if 1 <= s <= steps:
                 sine(s - 1)
             if s >= 2:
                 scale_and_store(s - 2)
-            if 1 <= s <= CHUNK_TILES:
-                quantise_row_tile(CHUNK_TILES + s - 1)
-            if s == CHUNK_TILES:
-                nc.vector.tensor_copy(out=w_and_p[:], in_=scalars[:, 2:4])
-            if s > CHUNK_TILES and (s - CHUNK_TILES) % 2 == 1 and (s - CHUNK_TILES) // 2 < ROW_TILES // LOAD_TILES:
-                linear_term(LOAD_TILES * ((s - CHUNK_TILES) // 2))
+            if s % 2 == 0 and s // 2 < LOADS:
+                linear_term(s // 2)
+            if s % 2 == 0 and 1 <= s // 2 <= LOADS:
+                store_linear(s // 2 - 1)

@@ -44,67 +44,6 @@ TINY = 1.2e-38
 FLOPS = 2 * ROWS * K * COLS
 
 
-def turn_back(nc, column, vector, angle, complement, tag):
-    sin_a = column("sin_" + tag)
-    cos_a = column("cos_" + tag)
-    nc.scalar.activation(out=sin_a[:], in_=angle[:], func=ACT.Sin)
-    nc.scalar.activation(out=cos_a[:], in_=complement[:], func=ACT.Sin)
-    across = column("across_" + tag)
-    along = column("along_" + tag)
-    nc.vector.tensor_mul(out=across[:], in0=vector["sine"][:], in1=sin_a[:])
-    nc.vector.scalar_tensor_tensor(
-        out=across[:], in0=cos_a[:], scalar=vector["abs_cosine"][:, 0:1], in1=across[:],
-        op0=ALU.mult, op1=ALU.subtract,
-    )
-    nc.vector.tensor_mul(out=along[:], in0=vector["sine"][:], in1=cos_a[:])
-    nc.vector.scalar_tensor_tensor(
-        out=along[:], in0=sin_a[:], scalar=vector["abs_cosine"][:, 0:1], in1=along[:], op0=ALU.mult, op1=ALU.add
-    )
-    return across, along
-
-
-def angle_of(nc, column, vector):
-    norm1 = column("norm1")
-    ratio = column("ratio")
-    guess = column("guess")
-    guess_complement = column("guess_complement")
-    nc.vector.tensor_scalar(
-        out=norm1[:], in0=vector["abs_sine"][:], scalar1=vector["abs_cosine"][:, 0:1], scalar2=TINY,
-        op0=ALU.add, op1=ALU.max,
-    )
-    nc.vector.reciprocal(out=norm1[:], in_=norm1[:])
-    nc.vector.tensor_mul(out=ratio[:], in0=vector["sine"][:], in1=norm1[:])
-    nc.vector.tensor_scalar(
-        out=guess[:], in0=ratio[:], scalar1=-HALF_PI, scalar2=HALF_PI, op0=ALU.mult, op1=ALU.add
-    )
-    nc.vector.tensor_scalar_mul(out=guess_complement[:], in0=ratio[:], scalar1=HALF_PI)
-
-    across, along = turn_back(nc, column, vector, guess, guess_complement, "guess")
-    tangent = column("tangent")
-    square = column("square")
-    series = column("series")
-    nc.vector.tensor_scalar_max(out=along[:], in0=along[:], scalar1=TINY)
-    nc.vector.reciprocal(out=along[:], in_=along[:])
-    nc.vector.tensor_mul(out=tangent[:], in0=across[:], in1=along[:])
-    nc.vector.tensor_mul(out=square[:], in0=tangent[:], in1=tangent[:])
-    nc.vector.tensor_scalar(
-        out=series[:], in0=square[:], scalar1=-1.0 / 7.0, scalar2=1.0 / 5.0, op0=ALU.mult, op1=ALU.add
-    )
-    for coefficient in (-1.0 / 3.0, 1.0):
-        nc.vector.tensor_scalar(
-            out=series[:], in0=series[:], scalar1=square[:, 0:1], scalar2=coefficient, op0=ALU.mult, op1=ALU.add
-        )
-    angle = column("angle")
-    complement = column("complement")
-    nc.vector.scalar_tensor_tensor(
-        out=angle[:], in0=series[:], scalar=tangent[:, 0:1], in1=guess[:], op0=ALU.mult, op1=ALU.add
-    )
-    nc.vector.tensor_scalar(
-        out=complement[:], in0=angle[:], scalar1=-1.0, scalar2=HALF_PI, op0=ALU.mult, op1=ALU.add
-    )
-    return angle, complement
-
-
 def tile_time2vec_kernel(tc, x, W_words, W_scales, P, w, p, sine_w, cosine_w, out):
     nc = tc.nc
     with ExitStack() as ctx:
@@ -139,6 +78,11 @@ def tile_time2vec_kernel(tc, x, W_words, W_scales, P, w, p, sine_w, cosine_w, ou
         nc.gpsimd.memset(scalar_row[:].bitcast(F32), 0.0)
         nc.gpsimd.memset(p_rows[:].bitcast(F32), 0.0)
         nc.gpsimd.memset(ones[:], 1.0)
+        signs = consts.tile([P128, 8], F32)
+        nc.gpsimd.memset(signs[:, 0:3], 1.0)
+        nc.gpsimd.memset(signs[:, 3:5], -1.0)
+        nc.gpsimd.memset(signs[:, 5:7], 0.0)
+        nc.gpsimd.memset(signs[:, 7:8], 1.0)
         for place, source, queue in (
             (0, sine_w, nc.sync), (2, w, nc.scalar), (1, cosine_w, nc.sync), (3, p, nc.scalar)
         ):
@@ -179,30 +123,84 @@ def tile_time2vec_kernel(tc, x, W_words, W_scales, P, w, p, sine_w, cosine_w, ou
         nc.vector.tensor_copy(
             out=scalars[:], in_=spread[:, SPREAD_SCALARS : SPREAD_SCALARS + len(SCALARS) * SCALAR_STEP : SCALAR_STEP]
         )
-        small = {}
-        for place, name in enumerate(SCALARS):
-            small[name] = scalars[:, place : place + 1]
 
-        vector = {"sine": small["sine"]}
-        for name, source in (("abs_sine", "sine"), ("abs_cosine", "cosine")):
-            vector[name] = column(name)
-            nc.vector.scalar_tensor_tensor(
-                out=vector[name][:], in0=small[source][:], scalar=-1.0, in1=small[source][:],
-                op0=ALU.mult, op1=ALU.max,
-            )
-        angle, complement = angle_of(nc, column, vector)
+        sine_col = scalars[:, 0:1]
+        cosine_col = scalars[:, 1:2]
+        magnitudes = consts.tile([P128, 2], F32)
+        signed_sine = consts.tile([P128, 4], F32)
+        norm1 = column("norm1")
         half_sign = column("half_sign")
+        quarters = consts.tile([P128, 4], F32)
+        trig = consts.tile([P128, 4], F32)
+        guess = column("guess")
+        part = consts.tile([P128, 2], F32)
+        turned = consts.tile([P128, 2], F32)
+        inverse = column("inverse")
+        half_tan = column("half_tan")
+        square = column("square")
+        series = column("series")
         phase = column("phase")
-        nc.vector.tensor_scalar(
-            out=half_sign[:], in0=small["cosine"][:], scalar1=0.0, scalar2=0.5, op0=ALU.is_ge, op1=ALU.subtract
-        )
-        nc.vector.tensor_scalar(
-            out=phase[:], in0=angle[:], scalar1=half_sign[:, 0:1], scalar2=2.0, op0=ALU.mult, op1=ALU.mult
-        )
+        root = column("root")
+        amplitude = column("amplitude")
         bias = consts.tile([P128, COL_TILES], F32)
         bias_turns = consts.tile([P128, COL_TILES], F32)
-        nc.vector.tensor_scalar_add(out=bias[:], in0=spread[:, 0:COL_TILES], scalar1=phase[:, 0:1])
-        nc.vector.tensor_scalar_mul(out=bias_turns[:], in0=bias[:], scalar1=1.0 / TWO_PI)
+
+        nc.vector.scalar_tensor_tensor(
+            out=magnitudes[:], in0=scalars[:, 0:2], scalar=-1.0, in1=scalars[:, 0:2], op0=ALU.mult, op1=ALU.max
+        )
+        nc.vector.tensor_scalar_mul(out=signed_sine[:], in0=signs[:, 0:4], scalar1=sine_col)
+        nc.vector.tensor_scalar(
+            out=norm1[:], in0=magnitudes[:, 0:1], scalar1=magnitudes[:, 1:2], scalar2=TINY, op0=ALU.add, op1=ALU.max
+        )
+        nc.vector.tensor_scalar(
+            out=half_sign[:], in0=cosine_col, scalar1=0.0, scalar2=0.5, op0=ALU.is_ge, op1=ALU.subtract
+        )
+        nc.vector.reciprocal(out=norm1[:], in_=norm1[:])
+        nc.vector.scalar_tensor_tensor(
+            out=quarters[:], in0=signed_sine[:], scalar=norm1[:, 0:1], in1=signs[:, 4:8], op0=ALU.mult, op1=ALU.add
+        )
+        nc.scalar.activation(out=trig[:], in_=quarters[:], func=ACT.Sin, scale=HALF_PI)
+        nc.vector.tensor_scalar(
+            out=guess[:], in0=quarters[:, 3:4], scalar1=half_sign[:, 0:1], scalar2=math.pi, op0=ALU.mult, op1=ALU.mult
+        )
+
+        def horner(out, coefficient):
+            nc.vector.tensor_scalar(
+                out=out[:], in0=out[:], scalar1=square[:, 0:1], scalar2=coefficient, op0=ALU.mult, op1=ALU.add
+            )
+
+        chain = [
+            lambda: nc.vector.tensor_scalar_mul(out=part[:], in0=trig[:, 0:2], scalar1=sine_col),
+            lambda: nc.vector.scalar_tensor_tensor(
+                out=turned[:], in0=trig[:, 2:4], scalar=magnitudes[:, 1:2], in1=part[:], op0=ALU.mult, op1=ALU.add
+            ),
+            lambda: nc.vector.tensor_scalar_max(out=inverse[:], in0=turned[:, 1:2], scalar1=TINY),
+            lambda: nc.vector.reciprocal(out=inverse[:], in_=inverse[:]),
+            lambda: nc.vector.scalar_tensor_tensor(
+                out=half_tan[:], in0=turned[:, 0:1], scalar=inverse[:, 0:1], in1=half_sign[:],
+                op0=ALU.mult, op1=ALU.mult,
+            ),
+            lambda: nc.vector.tensor_mul(out=square[:], in0=half_tan[:], in1=half_tan[:]),
+            lambda: nc.vector.tensor_scalar(
+                out=series[:], in0=square[:], scalar1=-128.0 / 7.0, scalar2=32.0 / 5.0, op0=ALU.mult, op1=ALU.add
+            ),
+            lambda: horner(series, -8.0 / 3.0),
+            lambda: horner(series, 2.0),
+            lambda: nc.vector.scalar_tensor_tensor(
+                out=phase[:], in0=series[:], scalar=half_tan[:, 0:1], in1=guess[:], op0=ALU.mult, op1=ALU.add
+            ),
+            lambda: nc.vector.tensor_scalar(
+                out=bias_turns[:], in0=spread[:, 0:COL_TILES], scalar1=phase[:, 0:1], scalar2=1.0 / TWO_PI,
+                op0=ALU.add, op1=ALU.mult,
+            ),
+            lambda: nc.vector.tensor_scalar_add(out=bias[:], in0=spread[:, 0:COL_TILES], scalar1=phase[:, 0:1]),
+            lambda: nc.vector.tensor_scalar(
+                out=root[:], in0=square[:], scalar1=4.0, scalar2=-2.0, op0=ALU.mult, op1=ALU.add
+            ),
+            lambda: horner(root, 2.0),
+            lambda: horner(root, 1.0),
+            lambda: nc.vector.tensor_mul(out=amplitude[:], in0=root[:], in1=turned[:, 1:2]),
+        ]
 
         for i in range(ROW_TILES):
             c, local = divmod(i, CHUNK_TILES)
@@ -221,8 +219,7 @@ def tile_time2vec_kernel(tc, x, W_words, W_scales, P, w, p, sine_w, cosine_w, ou
                     scales=x_planes[:, c, g, cols],
                     in_=grouped[:, g].rearrange("q b t -> q (b t)"),
                 )
-            if i == CHUNK_TILES - 1:
-                amplitude = turn_back(nc, column, vector, angle, complement, "angle")[1]
+                chain[PASSES * i + g]()
 
         w_and_p = consts.tile([P128, 2], F32)
         nc.vector.tensor_copy(out=w_and_p[:], in_=scalars[:, 2:4])

@@ -241,6 +241,7 @@ def tile_time2vec_kernel(tc, x, W_words, W_scales, P, w, p, sine_w, cosine_w, ou
 
         steps = CHUNKS * COL_TILES
         z_of = {}
+        turns_of = {}
         reduced_of = {}
         wave_of = {}
         back_of = {}
@@ -264,17 +265,19 @@ def tile_time2vec_kernel(tc, x, W_words, W_scales, P, w, p, sine_w, cosine_w, ou
                 )
             z_of[step] = z
 
-        def reduce_range(step):
+        def count_turns(step):
             j = step % COL_TILES
-            z = z_of[step]
             turns = work.tile([P128, CHUNK], I32)
             nc.vector.tensor_scalar(
-                out=turns[:], in0=z[:], scalar1=1.0 / TWO_PI, scalar2=bias_turns[:, j : j + 1],
+                out=turns[:], in0=z_of[step][:], scalar1=1.0 / TWO_PI, scalar2=bias_turns[:, j : j + 1],
                 op0=ALU.mult, op1=ALU.add,
             )
+            turns_of[step] = turns
+
+        def reduce_range(step):
             reduced = work.tile([P128, CHUNK], F32)
             nc.vector.scalar_tensor_tensor(
-                out=reduced[:], in0=turns[:], scalar=-TWO_PI, in1=z[:], op0=ALU.mult, op1=ALU.add
+                out=reduced[:], in0=turns_of[step][:], scalar=-TWO_PI, in1=z_of[step][:], op0=ALU.mult, op1=ALU.add
             )
             reduced_of[step] = reduced
 
@@ -312,11 +315,15 @@ def tile_time2vec_kernel(tc, x, W_words, W_scales, P, w, p, sine_w, cosine_w, ou
 
         multiply(0)
         multiply(1)
+        multiply(2)
+        count_turns(0)
         for s in range(steps + 2):
             if s >= 2:
                 turn_to_rows(s - 2)
-            if s + 2 < steps:
-                multiply(s + 2)
+            if s + 3 < steps:
+                multiply(s + 3)
+            if s + 1 < steps:
+                count_turns(s + 1)
             if s < steps:
                 reduce_range(s)
             if 1 <= s <= steps:

@@ -36,6 +36,7 @@ SCALARS = ("sine", "cosine", "w", "p")
 SCALAR_STEP = 16
 SPREAD_P = 32
 SPREAD_SCALARS = 64
+VECTOR_SCALES = (13, 14)
 
 HALF_PI = math.pi / 2.0
 TWO_PI = 2.0 * math.pi
@@ -305,10 +306,11 @@ def tile_time2vec_kernel(tc, x, W_words, W_scales, P, w, p, sine_w, cosine_w, ou
                 periodic = outgoing.tile([P128, CHUNK_TILES, STORE_TILES * P128], F32)
                 periodic_of[step // STORE_TILES] = periodic
             periodic = periodic_of[step // STORE_TILES]
-            nc.scalar.activation(
-                out=periodic[:, :, place * P128 : (place + 1) * P128], in_=back_of[step][:],
-                func=ACT.Copy, scale=amplitude[:, 0:1],
-            )
+            target = periodic[:, :, place * P128 : (place + 1) * P128]
+            if step in VECTOR_SCALES:
+                nc.vector.tensor_scalar_mul(out=target, in0=back_of[step][:], scalar1=amplitude[:, 0:1])
+            else:
+                nc.scalar.activation(out=target, in_=back_of[step][:], func=ACT.Copy, scale=amplitude[:, 0:1])
             if place == STORE_TILES - 1:
                 first = K + (j + 1 - STORE_TILES) * P128
                 nc.sync.dma_start(out=out_rows[:, tiles, first : first + STORE_TILES * P128], in_=periodic[:])

@@ -28,6 +28,8 @@ COL_TILES = COLS // P128
 STORE_TILES = 2
 LOAD_TILES = 2
 LOADS = ROW_TILES // LOAD_TILES
+LINEAR_TILES = 1
+LINEAR_PIECES = ROW_TILES // LINEAR_TILES
 PSUM_BANKS = 8
 W_LOADS = 2
 W_LOAD_COLS = COLS // W_LOADS
@@ -53,6 +55,7 @@ def tile_time2vec_kernel(tc, x, W_words, W_scales, P, w, p, sine_w, cosine_w, ou
         stage = ctx.enter_context(tc.tile_pool(name="stage", bufs=ROW_TILES))
         work = ctx.enter_context(tc.tile_pool(name="work", bufs=4))
         outgoing = ctx.enter_context(tc.tile_pool(name="outgoing", bufs=4))
+        lines = ctx.enter_context(tc.tile_pool(name="lines", bufs=LINEAR_PIECES))
         psum = ctx.enter_context(tc.psum_pool(name="psum", bufs=PSUM_BANKS))
         ctx.enter_context(tc.manual_schedule())
 
@@ -227,18 +230,18 @@ def tile_time2vec_kernel(tc, x, W_words, W_scales, P, w, p, sine_w, cosine_w, ou
 
         linear_of = {}
 
-        def linear_term(load):
-            tiles = slice(load * LOAD_TILES, (load + 1) * LOAD_TILES)
-            linear = outgoing.tile([P128, LOAD_TILES, K], F32)
+        def linear_term(piece):
+            tiles = slice(piece * LINEAR_TILES, (piece + 1) * LINEAR_TILES)
+            linear = lines.tile([P128, LINEAR_TILES, K], F32)
             nc.gpsimd.tensor_scalar(
                 out=linear[:], in0=x_sb[:, tiles, :],
                 scalar1=w_and_p[:, 0:1], scalar2=w_and_p[:, 1:2], op0=ALU.mult, op1=ALU.add,
             )
-            linear_of[load] = linear
+            linear_of[piece] = linear
 
-        def store_linear(load):
-            tiles = slice(load * LOAD_TILES, (load + 1) * LOAD_TILES)
-            nc.sync.dma_start(out=out_rows[:, tiles, 0:K], in_=linear_of[load][:])
+        def store_linear(piece):
+            tiles = slice(piece * LINEAR_TILES, (piece + 1) * LINEAR_TILES)
+            nc.sync.dma_start(out=out_rows[:, tiles, 0:K], in_=linear_of[piece][:])
 
         steps = CHUNKS * COL_TILES
         z_of = {}
@@ -330,9 +333,9 @@ def tile_time2vec_kernel(tc, x, W_words, W_scales, P, w, p, sine_w, cosine_w, ou
                 reduce_range(s)
             if 1 <= s <= steps:
                 sine(s - 1)
+            if s < LINEAR_PIECES:
+                linear_term(s)
+            if 1 <= s <= LINEAR_PIECES:
+                store_linear(s - 1)
             if s >= 2:
                 scale_and_store(s - 2)
-            if s % 2 == 0 and s // 2 < LOADS:
-                linear_term(s // 2)
-            if s % 2 == 0 and 1 <= s // 2 <= LOADS:
-                store_linear(s // 2 - 1)

@@ -30,6 +30,7 @@ LOAD_TILES = 2
 LOADS = ROW_TILES // LOAD_TILES
 LINEAR_TILES = 1
 LINEAR_PIECES = ROW_TILES // LINEAR_TILES
+SCALAR_PIECES = 2
 PSUM_BANKS = 8
 W_LOADS = 2
 W_LOAD_COLS = COLS // W_LOADS
@@ -233,10 +234,15 @@ def tile_time2vec_kernel(tc, x, W_words, W_scales, P, w, p, sine_w, cosine_w, ou
         def linear_term(piece):
             tiles = slice(piece * LINEAR_TILES, (piece + 1) * LINEAR_TILES)
             linear = lines.tile([P128, LINEAR_TILES, K], F32)
-            nc.gpsimd.tensor_scalar(
-                out=linear[:], in0=x_sb[:, tiles, :],
-                scalar1=w_and_p[:, 0:1], scalar2=w_and_p[:, 1:2], op0=ALU.mult, op1=ALU.add,
-            )
+            if piece < SCALAR_PIECES:
+                nc.scalar.activation(
+                    out=linear[:], in_=x_sb[:, tiles, :], func=ACT.Identity, scale=scalars[:, 2:3], bias=scalars[:, 3:4]
+                )
+            else:
+                nc.gpsimd.tensor_scalar(
+                    out=linear[:], in0=x_sb[:, tiles, :],
+                    scalar1=w_and_p[:, 0:1], scalar2=w_and_p[:, 1:2], op0=ALU.mult, op1=ALU.add,
+                )
             linear_of[piece] = linear
 
         def store_linear(piece):
@@ -318,6 +324,9 @@ def tile_time2vec_kernel(tc, x, W_words, W_scales, P, w, p, sine_w, cosine_w, ou
                 first = K + (j + 1 - STORE_TILES) * P128
                 nc.sync.dma_start(out=out_rows[:, tiles, first : first + STORE_TILES * P128], in_=periodic[:])
 
+        for piece in range(SCALAR_PIECES):
+            linear_term(piece)
+            store_linear(piece)
         multiply(0)
         multiply(1)
         multiply(2)
@@ -333,9 +342,9 @@ def tile_time2vec_kernel(tc, x, W_words, W_scales, P, w, p, sine_w, cosine_w, ou
                 reduce_range(s)
             if 1 <= s <= steps:
                 sine(s - 1)
-            if s < LINEAR_PIECES:
-                linear_term(s)
-            if 1 <= s <= LINEAR_PIECES:
-                store_linear(s - 1)
+            if SCALAR_PIECES + s < LINEAR_PIECES:
+                linear_term(SCALAR_PIECES + s)
+            if 1 <= s and SCALAR_PIECES + s - 1 < LINEAR_PIECES:
+                store_linear(SCALAR_PIECES + s - 1)
             if s >= 2:
                 scale_and_store(s - 2)

@@ -39,7 +39,7 @@ SCALARS = ("sine", "cosine", "w", "p")
 SCALAR_STEP = 16
 SPREAD_P = 32
 SPREAD_SCALARS = 64
-VECTOR_SCALES = (13, 14)
+VECTOR_SCALES = (12, 13, 14)
 
 HALF_PI = math.pi / 2.0
 TWO_PI = 2.0 * math.pi
@@ -320,7 +320,9 @@ def tile_time2vec_kernel(tc, x, W_words, W_scales, P, w, p, sine_w, cosine_w, ou
                 nc.vector.tensor_scalar_mul(out=target, in0=back_of[step][:], scalar1=amplitude[:, 0:1])
             else:
                 nc.scalar.activation(out=target, in_=back_of[step][:], func=ACT.Copy, scale=amplitude[:, 0:1])
-            if place == STORE_TILES - 1:
+            if step >= steps - STORE_TILES:
+                nc.sync.dma_start(out=out_rows[:, tiles, K + j * P128 : K + (j + 1) * P128], in_=target)
+            elif place == STORE_TILES - 1:
                 first = K + (j + 1 - STORE_TILES) * P128
                 nc.sync.dma_start(out=out_rows[:, tiles, first : first + STORE_TILES * P128], in_=periodic[:])
 
@@ -346,5 +348,8 @@ def tile_time2vec_kernel(tc, x, W_words, W_scales, P, w, p, sine_w, cosine_w, ou
                 linear_term(SCALAR_PIECES + s)
             if 1 <= s and SCALAR_PIECES + s - 1 < LINEAR_PIECES:
                 store_linear(SCALAR_PIECES + s - 1)
-            if s >= 2:
+            if s >= 2 and s - 2 not in VECTOR_SCALES:
                 scale_and_store(s - 2)
+            for step in VECTOR_SCALES:
+                if s == max(step + 2, steps - 1):
+                    scale_and_store(step)

@@ -307,6 +307,8 @@ def tile_time2vec_kernel(tc, x, W_words, W_scales, P, w, p, sine_w, cosine_w, ou
                 )
             back_of[step] = back
 
+        waiting = []
+
         def scale_and_store(step):
             c, j = divmod(step, COL_TILES)
             tiles = slice(c * CHUNK_TILES, (c + 1) * CHUNK_TILES)
@@ -324,7 +326,11 @@ def tile_time2vec_kernel(tc, x, W_words, W_scales, P, w, p, sine_w, cosine_w, ou
                 nc.sync.dma_start(out=out_rows[:, tiles, K + j * P128 : K + (j + 1) * P128], in_=target)
             elif place == STORE_TILES - 1:
                 first = K + (j + 1 - STORE_TILES) * P128
-                nc.sync.dma_start(out=out_rows[:, tiles, first : first + STORE_TILES * P128], in_=periodic[:])
+                rows = out_rows[:, tiles, first : first + STORE_TILES * P128]
+                if step in VECTOR_SCALES:
+                    nc.sync.dma_start(out=rows, in_=periodic[:])
+                else:
+                    waiting.append((rows, periodic))
 
         for piece in range(SCALAR_PIECES):
             linear_term(piece)
@@ -344,6 +350,9 @@ def tile_time2vec_kernel(tc, x, W_words, W_scales, P, w, p, sine_w, cosine_w, ou
                 reduce_range(s)
             if 1 <= s <= steps:
                 sine(s - 1)
+            for rows, periodic in waiting:
+                nc.scalar.dma_start(out=rows, in_=periodic[:])
+            waiting.clear()
             if SCALAR_PIECES + s < LINEAR_PIECES:
                 linear_term(SCALAR_PIECES + s)
             if 1 <= s and SCALAR_PIECES + s - 1 < LINEAR_PIECES:

import math
from contextlib import ExitStack

import concourse.mybir as mybir
from concourse.masks import make_identity

F32 = mybir.dt.float32
BF16 = mybir.dt.bfloat16
I32 = mybir.dt.int32
U32 = mybir.dt.uint32
U8 = mybir.dt.uint8
FP8X4 = mybir.dt.float8_e4m3fn_x4
ALU = mybir.AluOpType
ACT = mybir.ActivationFunctionType

P128 = 128
ROWS = 1024
K = 1024
COLS = 1024
PACK = 4
K_PASS = P128 * PACK
PASSES = K // K_PASS
ROW_TILES = ROWS // P128
CHUNK_TILES = 4
CHUNK = CHUNK_TILES * P128
CHUNKS = ROW_TILES // CHUNK_TILES
COL_TILES = COLS // P128
STORE_TILES = 2
LOAD_TILES = 2
LOADS = ROW_TILES // LOAD_TILES
LINEAR_TILES = 1
LINEAR_PIECES = ROW_TILES // LINEAR_TILES
SCALAR_PIECES = 2
PSUM_BANKS = 8
W_LOADS = 2
W_LOAD_COLS = COLS // W_LOADS
W_LOAD_TILES = COL_TILES // W_LOADS
SCALARS = ("sine", "cosine", "w", "p")
SCALAR_STEP = 16
SPREAD_P = 32
SPREAD_SCALARS = 64
VECTOR_SCALES = (12, 13, 14)

HALF_PI = math.pi / 2.0
TWO_PI = 2.0 * math.pi
TINY = 1.2e-38

FLOPS = 2 * ROWS * K * COLS


def tile_time2vec_kernel(tc, x, W_words, W_scales, P, w, p, sine_w, cosine_w, out):
    nc = tc.nc
    with ExitStack() as ctx:
        consts = ctx.enter_context(tc.tile_pool(name="consts", bufs=1))
        keep = ctx.enter_context(tc.tile_pool(name="keep", bufs=1))
        stage = ctx.enter_context(tc.tile_pool(name="stage", bufs=ROW_TILES))
        work = ctx.enter_context(tc.tile_pool(name="work", bufs=4))
        outgoing = ctx.enter_context(tc.tile_pool(name="outgoing", bufs=4))
        lines = ctx.enter_context(tc.tile_pool(name="lines", bufs=LINEAR_PIECES))
        psum = ctx.enter_context(tc.psum_pool(name="psum", bufs=PSUM_BANKS))
        ctx.enter_context(tc.manual_schedule())

        def column(name):
            return consts.tile([P128, 1], F32, name=name)

        x_rows = x.rearrange("(p i) k -> p i k", i=ROW_TILES)
        out_rows = out.rearrange("(p i) c -> p i c", i=ROW_TILES)

        x_sb = keep.tile([P128, ROW_TILES, K], BF16)
        x_pairs = x_sb[:].bitcast(F32)
        w_codes = keep.tile([P128, W_LOADS, PASSES, W_LOAD_COLS], U32, align_bytes=64)
        w_planes = keep.tile([P128, PASSES, COLS], U8, align_bytes=64)
        x_codes = keep.tile([P128, CHUNKS, PASSES, CHUNK], U32, align_bytes=64)
        x_planes = keep.tile([P128, CHUNKS, PASSES, CHUNK], U8, align_bytes=64)

        nc.vector.memset(w_planes[:].bitcast(I32), 0)
        zero = column("zero")
        nc.vector.memset(zero[:], 0.0)

        p_rows = consts.tile([P128, P128], BF16)
        scalar_row = consts.tile([P128, len(SCALARS) * SCALAR_STEP], BF16)
        ones = consts.tile([P128, P128], BF16)
        nc.gpsimd.memset(scalar_row[:].bitcast(F32), 0.0)
        nc.gpsimd.memset(p_rows[:].bitcast(F32), 0.0)
        nc.gpsimd.memset(ones[:], 1.0)
        signs = consts.tile([P128, 8], F32)
        nc.gpsimd.memset(signs[:, 0:3], 1.0)
        nc.gpsimd.memset(signs[:, 3:5], -1.0)
        nc.gpsimd.memset(signs[:, 5:7], 0.0)
        nc.gpsimd.memset(signs[:, 7:8], 1.0)
        for place, source, queue in (
            (0, sine_w, nc.sync), (2, w, nc.scalar), (1, cosine_w, nc.sync), (3, p, nc.scalar)
        ):
            queue.dma_start(
                out=scalar_row[0:1, place * SCALAR_STEP : place * SCALAR_STEP + 1],
                in_=source.rearrange("(o n) -> o n", o=1),
            )
        nc.sync.dma_start(out=p_rows[0:COL_TILES, :], in_=P.rearrange("(j n) -> j n", n=P128))

        for first_tile in range(0, ROW_TILES, LOAD_TILES):
            tiles = slice(first_tile, first_tile + LOAD_TILES)
            nc.sync.dma_start(out=x_sb[:, tiles, :], in_=x_rows[:, tiles, :])
        for quadrant in range(4):
            nc.sync.dma_start(
                out=w_planes[32 * quadrant : 32 * quadrant + 4].bitcast(I32),
                in_=W_scales[:, 4 * quadrant : 4 * quadrant + 4, :].rearrange("g r n -> r g n").bitcast(I32),
            )
        w_words = W_words.rearrange("g q n t -> q g (n t)").bitcast(I32)
        for part in range(W_LOADS):
            cols = slice(part * W_LOAD_COLS, (part + 1) * W_LOAD_COLS)
            nc.sync.dma_start(out=w_codes[:, part].bitcast(I32), in_=w_words[:, :, cols])

        table_warm = column("table_warm")
        nc.scalar.activation(out=table_warm[:], in_=zero[:], func=ACT.Sin)

        identity = consts.tile([P128, P128], F32)
        make_identity(nc, identity[:])

        identity_bf = consts.tile([P128, SPREAD_P], BF16)
        nc.vector.tensor_copy(out=identity_bf[:], in_=identity[:, 0:SPREAD_P])
        spread = psum.tile([P128, CHUNK], F32, tag="bank")
        nc.tensor.matmul(
            out=spread[:, SPREAD_SCALARS : SPREAD_SCALARS + len(SCALARS) * SCALAR_STEP],
            lhsT=ones[:], rhs=scalar_row[:], start=True, stop=True,
        )
        nc.tensor.matmul(out=spread[:, 0:SPREAD_P], lhsT=p_rows[:], rhs=identity_bf[:], start=True, stop=True)
        scalars = consts.tile([P128, len(SCALARS)], F32)
        nc.vector.tensor_copy(
            out=scalars[:], in_=spread[:, SPREAD_SCALARS : SPREAD_SCALARS + len(SCALARS) * SCALAR_STEP : SCALAR_STEP]
        )

        sine_col = scalars[:, 0:1]
        cosine_col = scalars[:, 1:2]
        magnitudes = consts.tile([P128, 2], F32)
        signed_sine = consts.tile([P128, 4], F32)
        norm1 = column("norm1")
        half_sign = column("half_sign")
        quarters = consts.tile([P128, 4], F32)
        trig = consts.tile([P128, 4], F32)
        guess = column("guess")
        part = consts.tile([P128, 2], F32)
        turned = consts.tile([P128, 2], F32)
        inverse = column("inverse")
        half_tan = column("half_tan")
        square = column("square")
        series = column("series")
        phase = column("phase")
        root = column("root")
        amplitude = column("amplitude")
        bias = consts.tile([P128, COL_TILES], F32)
        bias_turns = consts.tile([P128, COL_TILES], F32)

        nc.vector.scalar_tensor_tensor(
            out=magnitudes[:], in0=scalars[:, 0:2], scalar=-1.0, in1=scalars[:, 0:2], op0=ALU.mult, op1=ALU.max
        )
        nc.vector.tensor_scalar_mul(out=signed_sine[:], in0=signs[:, 0:4], scalar1=sine_col)
        nc.vector.tensor_scalar(
            out=norm1[:], in0=magnitudes[:, 0:1], scalar1=magnitudes[:, 1:2], scalar2=TINY, op0=ALU.add, op1=ALU.max
        )
        nc.vector.tensor_scalar(
            out=half_sign[:], in0=cosine_col, scalar1=0.0, scalar2=0.5, op0=ALU.is_ge, op1=ALU.subtract
        )
        nc.vector.reciprocal(out=norm1[:], in_=norm1[:])
        nc.vector.scalar_tensor_tensor(
            out=quarters[:], in0=signed_sine[:], scalar=norm1[:, 0:1], in1=signs[:, 4:8], op0=ALU.mult, op1=ALU.add
        )
        nc.scalar.activation(out=trig[:], in_=quarters[:], func=ACT.Sin, scale=HALF_PI)
        nc.vector.tensor_scalar(
            out=guess[:], in0=quarters[:, 3:4], scalar1=half_sign[:, 0:1], scalar2=math.pi, op0=ALU.mult, op1=ALU.mult
        )

        def horner(out, coefficient):
            nc.vector.tensor_scalar(
                out=out[:], in0=out[:], scalar1=square[:, 0:1], scalar2=coefficient, op0=ALU.mult, op1=ALU.add
            )

        chain = [
            lambda: nc.vector.tensor_scalar_mul(out=part[:], in0=trig[:, 0:2], scalar1=sine_col),
            lambda: nc.vector.scalar_tensor_tensor(
                out=turned[:], in0=trig[:, 2:4], scalar=magnitudes[:, 1:2], in1=part[:], op0=ALU.mult, op1=ALU.add
            ),
            lambda: nc.vector.tensor_scalar_max(out=inverse[:], in0=turned[:, 1:2], scalar1=TINY),
            lambda: nc.vector.reciprocal(out=inverse[:], in_=inverse[:]),
            lambda: nc.vector.scalar_tensor_tensor(
                out=half_tan[:], in0=turned[:, 0:1], scalar=inverse[:, 0:1], in1=half_sign[:],
                op0=ALU.mult, op1=ALU.mult,
            ),
            lambda: nc.vector.tensor_mul(out=square[:], in0=half_tan[:], in1=half_tan[:]),
            lambda: nc.vector.tensor_scalar(
                out=series[:], in0=square[:], scalar1=-128.0 / 7.0, scalar2=32.0 / 5.0, op0=ALU.mult, op1=ALU.add
            ),
            lambda: horner(series, -8.0 / 3.0),
            lambda: horner(series, 2.0),
            lambda: nc.vector.scalar_tensor_tensor(
                out=phase[:], in0=series[:], scalar=half_tan[:, 0:1], in1=guess[:], op0=ALU.mult, op1=ALU.add
            ),
            lambda: nc.vector.tensor_scalar(
                out=bias_turns[:], in0=spread[:, 0:COL_TILES], scalar1=phase[:, 0:1], scalar2=1.0 / TWO_PI,
                op0=ALU.add, op1=ALU.mult,
            ),
            lambda: nc.vector.tensor_scalar_add(out=bias[:], in0=spread[:, 0:COL_TILES], scalar1=phase[:, 0:1]),
            lambda: nc.vector.tensor_scalar(
                out=root[:], in0=square[:], scalar1=4.0, scalar2=-2.0, op0=ALU.mult, op1=ALU.add
            ),
            lambda: horner(root, 2.0),
            lambda: horner(root, 1.0),
            lambda: nc.vector.tensor_mul(out=amplitude[:], in0=root[:], in1=turned[:, 1:2]),
        ]

        for i in range(ROW_TILES):
            c, local = divmod(i, CHUNK_TILES)
            cols = slice(local * P128, (local + 1) * P128)
            xt = psum.tile([P128, PACK, P128], F32, tag="bank")
            for g in range(PASSES):
                for u in range(2):
                    nc.tensor.transpose(
                        xt[:, 2 * g + u, :], x_pairs[:, i, 256 * g + u : 256 * (g + 1) : 2], identity[:]
                    )
            grouped = stage.tile([P128, PASSES, P128, PACK], BF16, align_bytes=64)
            nc.scalar.copy(out=grouped[:].bitcast(F32), in_=xt[:].rearrange("q (g u) b -> q g b u", u=2))
            for g in range(PASSES):
                nc.vector.quantize_mx(
                    out=x_codes[:, c, g, cols].bitcast(FP8X4),
                    scales=x_planes[:, c, g, cols],
                    in_=grouped[:, g].rearrange("q b t -> q (b t)"),
                )
                chain[PASSES * i + g]()

        w_and_p = consts.tile([P128, 2], F32)
        nc.vector.tensor_copy(out=w_and_p[:], in_=scalars[:, 2:4])

        linear_of = {}

        def linear_term(piece):
            tiles = slice(piece * LINEAR_TILES, (piece + 1) * LINEAR_TILES)
            linear = lines.tile([P128, LINEAR_TILES, K], F32)
            if piece < SCALAR_PIECES:
                nc.scalar.activation(
                    out=linear[:], in_=x_sb[:, tiles, :], func=ACT.Identity, scale=scalars[:, 2:3], bias=scalars[:, 3:4]
                )
            else:
                nc.gpsimd.tensor_scalar(
                    out=linear[:], in0=x_sb[:, tiles, :],
                    scalar1=w_and_p[:, 0:1], scalar2=w_and_p[:, 1:2], op0=ALU.mult, op1=ALU.add,
                )
            linear_of[piece] = linear

        def store_linear(piece):
            tiles = slice(piece * LINEAR_TILES, (piece + 1) * LINEAR_TILES)
            nc.sync.dma_start(out=out_rows[:, tiles, 0:K], in_=linear_of[piece][:])

        steps = CHUNKS * COL_TILES
        z_of = {}
        turns_of = {}
        reduced_of = {}
        wave_of = {}
        back_of = {}
        periodic_of = {}

        def multiply(step):
            c, j = divmod(step, COL_TILES)
            n_cols = slice(j * P128, (j + 1) * P128)
            part, part_tile = divmod(j, W_LOAD_TILES)
            part_cols = slice(part_tile * P128, (part_tile + 1) * P128)
            z = psum.tile([P128, CHUNK], F32, tag="bank")
            for g in range(PASSES):
                nc.tensor.matmul_mx(
                    out=z[:],
                    lhsT=w_codes[:, part, g, part_cols].bitcast(FP8X4),
                    lhsT_scale=w_planes[:, g, n_cols],
                    rhs=x_codes[:, c, g, :].bitcast(FP8X4),
                    rhs_scale=x_planes[:, c, g, :],
                    start=(g == 0),
                    stop=(g == PASSES - 1),
                )
            z_of[step] = z

        def count_turns(step):
            j = step % COL_TILES
            turns = work.tile([P128, CHUNK], I32)
            nc.vector.tensor_scalar(
                out=turns[:], in0=z_of[step][:], scalar1=1.0 / TWO_PI, scalar2=bias_turns[:, j : j + 1],
                op0=ALU.mult, op1=ALU.add,
            )
            turns_of[step] = turns

        def reduce_range(step):
            reduced = work.tile([P128, CHUNK], F32)
            nc.vector.scalar_tensor_tensor(
                out=reduced[:], in0=turns_of[step][:], scalar=-TWO_PI, in1=z_of[step][:], op0=ALU.mult, op1=ALU.add
            )
            reduced_of[step] = reduced

        def sine(step):
            j = step % COL_TILES
            wave = work.tile([P128, CHUNK], F32)
            nc.scalar.activation(
                out=wave[:], in_=reduced_of[step][:], func=ACT.Sin, bias=bias[:, j : j + 1], scale=1.0
            )
            wave_of[step] = wave

        def turn_to_rows(step):
            back = psum.tile([P128, CHUNK_TILES, P128], F32, tag="bank")
            for local in range(CHUNK_TILES):
                nc.tensor.transpose(
                    back[:, local, :], wave_of[step][:, local * P128 : (local + 1) * P128], identity[:]
                )
            back_of[step] = back

        waiting = []

        def scale_and_store(step):
            c, j = divmod(step, COL_TILES)
            tiles = slice(c * CHUNK_TILES, (c + 1) * CHUNK_TILES)
            place = j % STORE_TILES
            if place == 0:
                periodic = outgoing.tile([P128, CHUNK_TILES, STORE_TILES * P128], F32)
                periodic_of[step // STORE_TILES] = periodic
            periodic = periodic_of[step // STORE_TILES]
            target = periodic[:, :, place * P128 : (place + 1) * P128]
            if step in VECTOR_SCALES:
                nc.vector.tensor_scalar_mul(out=target, in0=back_of[step][:], scalar1=amplitude[:, 0:1])
            else:
                nc.scalar.activation(out=target, in_=back_of[step][:], func=ACT.Copy, scale=amplitude[:, 0:1])
            if step >= steps - STORE_TILES:
                nc.sync.dma_start(out=out_rows[:, tiles, K + j * P128 : K + (j + 1) * P128], in_=target)
            elif place == STORE_TILES - 1:
                first = K + (j + 1 - STORE_TILES) * P128
                rows = out_rows[:, tiles, first : first + STORE_TILES * P128]
                if step in VECTOR_SCALES:
                    nc.sync.dma_start(out=rows, in_=periodic[:])
                else:
                    waiting.append((rows, periodic))

        for piece in range(SCALAR_PIECES):
            linear_term(piece)
            store_linear(piece)
        multiply(0)
        multiply(1)
        multiply(2)
        count_turns(0)
        for s in range(steps + 2):
            if s >= 2:
                turn_to_rows(s - 2)
            if s + 3 < steps:
                multiply(s + 3)
            if s + 1 < steps:
                count_turns(s + 1)
            if s < steps:
                reduce_range(s)
            if 1 <= s <= steps:
                sine(s - 1)
            for rows, periodic in waiting:
                nc.scalar.dma_start(out=rows, in_=periodic[:])
            waiting.clear()
            if SCALAR_PIECES + s < LINEAR_PIECES:
                linear_term(SCALAR_PIECES + s)
            if 1 <= s and SCALAR_PIECES + s - 1 < LINEAR_PIECES:
                store_linear(SCALAR_PIECES + s - 1)
            if s >= 2 and s - 2 not in VECTOR_SCALES:
                scale_and_store(s - 2)
            for step in VECTOR_SCALES:
                if s == max(step + 2, steps - 1):
                    scale_and_store(step)
